import numpy as np
import ml_dtypes


def mxq(x, axis, fmt="e4m3"):
    dtype, down = {"e4m3": (ml_dtypes.float8_e4m3fn, 7), "e5m2": (ml_dtypes.float8_e5m2, 14)}[fmt]
    v = np.moveaxis(np.asarray(x, np.float32).astype(ml_dtypes.bfloat16).astype(np.float64), axis, -1)
    blocks = v.reshape(v.shape[:-1] + (-1, 32))
    amax = np.abs(blocks).max(-1, keepdims=True)
    byte = np.maximum(np.where(amax > 0, np.frexp(amax)[1] - 1 + 127, 0) - down, 1)
    scale = np.exp2(byte - 127.0)
    codes = (blocks / scale).astype(np.float32).astype(dtype).astype(np.float64)
    return np.moveaxis((codes * scale).reshape(v.shape), -1, axis)


WIDE = False


def mx_kscale(k):
    if not WIDE:
        return np.ones(k)
    levels = np.array([18, -18])
    if k % 512:
        return np.exp2(np.random.permutation(np.resize(levels, k // 32))).repeat(32)
    a = np.empty((k // 512, 16))
    for p in range(k // 512):
        a[p, :8] = np.random.permutation(np.resize(levels, 8))
        for g in range(8):
            far = levels[np.abs(levels - a[p, g]) >= 10]
            a[p, g + 8] = far[np.random.randint(len(far))]
    return np.exp2(a.ravel()).repeat(32)


BF16 = ml_dtypes.bfloat16


def bf(x):
    return np.asarray(x, np.float32).astype(BF16)


def f64(x):
    return np.asarray(x).astype(np.float64)


B, S, D, H, KV, HD = 1, 1024, 1024, 8, 4, 128
THETA = 10000.0
HALF = HD // 2


def angles():
    inv_freq = 1.0 / (THETA ** (np.arange(0.0, HD, 2.0) / HD))
    return np.arange(0.0, S)[:, None] * inv_freq[None, :]


def rope(x, cos, sin):
    xr, xi = x[..., :HALF], x[..., HALF:]
    return np.concatenate([xr * cos - xi * sin, xr * sin + xi * cos], axis=-1)


def rope_back(g, cos, sin):
    gr, gi = g[..., :HALF], g[..., HALF:]
    return np.concatenate([gr * cos + gi * sin, gi * cos - gr * sin], axis=-1)


def rows(g):
    return g.transpose(0, 2, 1, 3).reshape(S, -1)


def pair_scale(heads):
    u = mx_kscale(heads * HD).reshape(heads, 2, HALF)[:, 0, :]
    return np.concatenate([u, u], axis=-1)


def draw_grad(heads, s, u):
    n = np.random.standard_normal((B, heads, S, HD))
    e = np.exp2(np.random.randint(-6, 1, (B, 1, S, 1)))
    return bf(n * e / s[None, None, :, None] * u[None, :, None, :])


def setup_inputs():
    s = mx_kscale(S)
    uq = pair_scale(H)
    uk = pair_scale(KV)
    uv = mx_kscale(KV * HD).reshape(KV, HD)
    hidden_states = bf(np.random.standard_normal((B, S, D)) * s[None, :, None])
    Wq = bf(np.random.standard_normal((D, H * HD)) * 1.2 / np.sqrt(D) / uq.reshape(-1)[None, :])
    Wk = bf(np.random.standard_normal((D, KV * HD)) * 1.2 / np.sqrt(D) / uk.reshape(-1)[None, :])
    Wv = bf(np.random.standard_normal((D, KV * HD)) * 1.5 / np.sqrt(D) / uv.reshape(-1)[None, :])
    grad_0 = draw_grad(H, s, uq)
    grad_1 = draw_grad(KV, s, uk)
    grad_2 = draw_grad(KV, s, uv)
    return {"hidden_states": hidden_states, "Wq": Wq, "Wk": Wk, "Wv": Wv,
            "grad_0": grad_0, "grad_1": grad_1, "grad_2": grad_2}


def reference(hidden_states, Wq, Wk, Wv, grad_0, grad_1, grad_2):
    a = angles()
    cos = np.cos(a)[None, None]
    sin = np.sin(a)[None, None]
    dq = rows(rope_back(f64(grad_0), cos, sin))
    dk = rows(rope_back(f64(grad_1), cos, sin))
    dv = rows(f64(grad_2))
    dz = np.concatenate([dq, dk, dv], axis=1)
    w = np.concatenate([f64(Wq), f64(Wk), f64(Wv)], axis=1)
    x = f64(hidden_states).reshape(S, D)
    dx = mxq(dz, 1, "e5m2") @ mxq(w, 1, "e4m3").T
    dw = mxq(x, 0, "e4m3").T @ mxq(dz, 0, "e5m2")
    nq, nk = H * HD, KV * HD
    return dx.reshape(B, S, D), dw[:, :nq], dw[:, nq:nq + nk], dw[:, nq + nk:]

@@ -1,0 +1,419 @@
+import math
+from contextlib import ExitStack
+
+import concourse.mybir as mybir
+from concourse.masks import make_identity
+
+S, D, HD = 1024, 1024, 128
+J = 2048
+HALF = HD // 2
+THETA = 10000.0
+FLOPS = 2 * 2 * S * D * J
+
+F32 = mybir.dt.float32
+BF16 = mybir.dt.bfloat16
+I32 = mybir.dt.int32
+U32 = mybir.dt.uint32
+U8 = mybir.dt.uint8
+E4 = mybir.dt.float8_e4m3fn_x4
+E5 = mybir.dt.float8_e5m2_x4
+ALU = mybir.AluOpType
+ACT = mybir.ActivationFunctionType
+
+P = 128
+QA, QB, KK, VV = 0, 1, 2, 3
+
+
+def tile_ringattention_pa_v_kernel(tc, hidden_states, Wq, Wk, Wv, grad_0, grad_1, grad_2,
+                                                out_0, out_1, out_2, out_3):
+    nc = tc.nc
+    with ExitStack() as ctx:
+        keep = ctx.enter_context(tc.tile_pool(name="keep", bufs=1))
+        work = ctx.enter_context(tc.tile_pool(name="work", bufs=2))
+        psum = ctx.enter_context(tc.psum_pool(name="psum", bufs=1))
+        ctx.enter_context(tc.manual_schedule())
+
+        raw_g, raw_x, raw_w, nat = {}, {}, {}, {}
+        grads = {QA: (grad_0, 0), QB: (grad_0, 4), KK: (grad_1, 0), VV: (grad_2, 0)}
+
+        def load_g(g, c):
+            src, h0 = grads[c]
+            tl = work.tile([P, 2048], BF16, name="raw_g", tag="raw_g", bufs=4)
+            nc.sync.dma_start(out=tl[:].rearrange("p (h w) -> p h w", h=4),
+                              in_=src[0, h0:h0 + 4, 512 * g:512 * (g + 1), :].rearrange("h (p t) d -> p h (t d)", t=4))
+            raw_g[(g, c)] = tl
+
+        def load_v(g):
+            tl = keep.tile([P, 2048], BF16, name="nat_v%d" % g, align_bytes=64)
+            for h in range(4):
+                nc.sync.dma_start(out=tl[:].rearrange("p (t h d) -> p t h d", t=4, h=4)[:, :, h, :],
+                                  in_=grad_2[0, h, 512 * g:512 * (g + 1), :].rearrange("(p t) d -> p t d", t=4))
+            nat[(g, VV)] = tl
+
+        def load_x(g):
+            tl = keep.tile([P, 4096], BF16, name="raw_x%d" % g)
+            nc.sync.dma_start(out=tl[:], in_=hidden_states[0, 512 * g:512 * (g + 1), :].rearrange("(p t) d -> p (t d)", t=4))
+            raw_x[g] = tl
+
+        def load_w(src, name, rows, chunks):
+            n = (rows.stop - rows.start) // P
+            width = 512 * len(chunks)
+            tl = keep.tile([P, n * width], BF16, name=name)
+            nc.sync.dma_start(out=tl[:].rearrange("p (a w) -> p a w", a=n),
+                              in_=src[rows, :].rearrange("(a p) w -> p a w", p=P))
+            for a in range(n):
+                for i, c in enumerate(chunks):
+                    raw_w[(c, rows.start // P + a)] = tl[:, a * width + 512 * i:a * width + 512 * (i + 1)]
+
+        def load_wv():
+            load_w(Wv, "raw_wv", slice(0, D), [VV])
+
+        def load_wk():
+            load_w(Wk, "raw_wk", slice(0, D), [KK])
+
+        def load_wq(h):
+            load_w(Wq, "raw_wq%d" % h, slice(512 * h, 512 * (h + 1)), [QA, QB])
+
+        ident = keep.tile([P, P], F32)
+        table = [keep.tile([P, 4, 2, HALF], F32, name="table%d" % g) for g in range(2)]
+
+        def tables():
+            ones = keep.tile([P, 8], F32)
+            nc.vector.memset(ones[:], 1.0)
+            warm = keep.tile([P, 1], F32)
+            nc.scalar.activation(out=warm[:], in_=ones[:, 0:1], func=ACT.Sin)
+            tok = keep.tile([P, 8], F32)
+            nc.gpsimd.iota(tok[:], pattern=[[512, 2], [1, 4]], base=0, channel_multiplier=4, allow_small_or_imprecise_dtypes=True)
+            make_identity(nc, ident[:])
+            freq = keep.tile([P, HALF], F32)
+            for b in range(8):
+                nc.vector.tensor_scalar(out=freq[:, b:b + 1], in0=ones[:, b:b + 1], scalar1=THETA ** (-b / HALF) / (2 * math.pi),
+                                        scalar2=None, op0=ALU.mult)
+            for a in range(1, 8):
+                nc.vector.tensor_scalar(out=freq[:, 8 * a:8 * a + 8], in0=freq[:, 0:8], scalar1=THETA ** (-8 * a / HALF),
+                                        scalar2=None, op0=ALU.mult)
+            whole = work.tile([P, 1024], I32, name="whole", tag="res", bufs=5)
+            frac = work.tile([P, 1024], F32, name="frac", tag="res", bufs=5)
+            for g in range(2):
+                for i in range(4 * g, 4 * g + 4):
+                    nc.vector.tensor_scalar(out=whole[:, HALF * i:HALF * (i + 1)], in0=freq[:], scalar1=tok[:, i:i + 1],
+                                            scalar2=None, op0=ALU.mult)
+                for i in range(4 * g, 4 * g + 4):
+                    nc.vector.scalar_tensor_tensor(out=frac[:, HALF * i:HALF * (i + 1)], in0=freq[:], scalar=tok[:, i:i + 1],
+                                                   in1=whole[:, HALF * i:HALF * (i + 1)], op0=ALU.mult, op1=ALU.subtract)
+                r = frac[:, 256 * g:256 * (g + 1)]
+                mag = frac[:, 512 + 256 * g:512 + 256 * (g + 1)]
+                nc.scalar.activation(out=mag, in_=r, func=ACT.Abs)
+                nc.scalar.activation(out=table[g][:, :, 0, :], in_=mag.rearrange("p (t j) -> p t j", t=4), func=ACT.Sin,
+                                     scale=-2 * math.pi, bias=math.pi / 2)
+                nc.scalar.activation(out=table[g][:, :, 1, :], in_=r.rearrange("p (t j) -> p t j", t=4), func=ACT.Sin,
+                                     scale=2 * math.pi)
+
+        turn_ring, mm_ring = [0, 1], [2, 3, 4, 5, 6, 7]
+
+        def take_bank(ring, hold=False):
+            b = ring[0]
+            ring.remove(b)
+            if not hold:
+                ring.append(b)
+            return psum.tile([P, 512], F32, name="bank%d" % b, tag="bank%d" % b), b
+
+        def mx_tiles(name, width):
+            codes = keep.tile([P, width], U32, name=name + "_c", align_bytes=64)
+            scales = keep.tile([P, width], U8, name=name + "_s", align_bytes=64)
+            return codes, scales
+
+        tok_major = {(g, c): mx_tiles("a%d%d" % (g, c), 512) for g in range(2) for c in range(4)}
+        feat_major = {(g, c, h): mx_tiles("b%d%d%d" % (g, c, h), 256) for g in range(2) for c in range(4) for h in range(2)}
+        w_mx = {(c, h): mx_tiles("w%d%d" % (c, h), 512) for c in range(4) for h in range(2)}
+        x_mx = {(g, h): mx_tiles("x%d%d" % (g, h), 512) for g in range(2) for h in range(2)}
+        prod, st_a, st_b, st_w = {}, {}, {}, {}
+
+        def copy(eng, out, in_):
+            if eng == "v":
+                nc.vector.tensor_copy(out=out, in_=in_)
+            else:
+                nc.scalar.copy(out=out, in_=in_)
+
+        def mult(g, c, t):
+            if t % 2 == 0:
+                prod[(g, c, t // 2)] = work.tile([P, 2048], F32, name="prod", tag="prod", bufs=2)
+            tl = prod[(g, c, t // 2)]
+            gr = raw_g[(g, c)][:].rearrange("p (h t d) -> p t h d", h=4, t=4)[:, t, :, :]
+            nc.vector.tensor_tensor(
+                out=tl[:, 1024 * (t % 2):1024 * (t % 2 + 1)].rearrange("p (s h d) -> p s h d", s=2, h=4),
+                in0=gr.unsqueeze(1).to_broadcast([P, 2, 4, HD]),
+                in1=table[g][:, t, :, :].unsqueeze(2).to_broadcast([P, 2, 8, HALF]),
+                op=ALU.mult)
+
+        def add(g, c, pair):
+            if pair == 0:
+                nat[(g, c)] = work.tile([P, 2048], BF16, name="nat", tag="nat", bufs=4, align_bytes=64)
+            dst = nat[(g, c)][:, 1024 * pair:1024 * (pair + 1)].rearrange("p (t h s j) -> p t h s j", t=2, h=4, s=2)
+            m = prod[(g, c, pair)][:].rearrange("p (t f h s j) -> p t f h s j", t=2, f=2, h=4, s=2)
+            nc.vector.tensor_tensor(out=dst[:, :, :, 0, :], in0=m[:, :, 0, :, 0, :], in1=m[:, :, 1, :, 1, :], op=ALU.add)
+            nc.vector.tensor_tensor(out=dst[:, :, :, 1, :], in0=m[:, :, 0, :, 1, :], in1=m[:, :, 1, :, 0, :], op=ALU.subtract)
+
+        def turn(srcs, dst):
+            bank = take_bank(turn_ring)[0]
+            for a in range(2):
+                words = srcs[a].bitcast(F32)
+                for u in range(2):
+                    nc.tensor.transpose(bank[:, 256 * a + 128 * u:256 * a + 128 * (u + 1)], words[:, u:256:2], ident[:])
+            nc.scalar.copy(out=dst.bitcast(F32).rearrange("p (a r u) -> p a r u", a=2, u=2),
+                           in_=bank[:].rearrange("p (a u r) -> p a r u", a=2, u=2))
+
+        def turn_dz(g, c, pair):
+            tl = work.tile([P, 1024], BF16, name="st_b", tag="st_b", bufs=4, align_bytes=64)
+            st_b[(g, c, pair)] = tl
+            turn([nat[(g, c)][:, 512 * t:512 * (t + 1)] for t in (2 * pair, 2 * pair + 1)], tl[:])
+
+        def turn_w(c, h):
+            tl = work.tile([P, 2048], BF16, name="st_w", tag="st_w", bufs=3, align_bytes=64)
+            st_w[(c, h)] = tl
+            for b in range(2):
+                turn([raw_w[(c, 4 * h + 2 * b + a)] for a in range(2)], tl[:, 1024 * b:1024 * (b + 1)])
+
+        def weave(eng, key, src):
+            tl = work.tile([P, 2048], BF16, name="st_a", tag="st_a", bufs=3, align_bytes=64)
+            st_a[key] = tl
+            copy(eng, tl[:].rearrange("p (c i t) -> p c t i", i=4, t=4), src.rearrange("p t (c i) -> p c t i", i=4))
+
+        def weave_dz(eng, g, c):
+            weave(eng, (g, c), nat[(g, c)][:].rearrange("p (t f) -> p t f", t=4))
+
+        def weave_x(eng, g, h):
+            weave(eng, ("x", g, h), raw_x[g][:].rearrange("p (t f) -> p t f", t=4)[:, :, 512 * h:512 * (h + 1)])
+
+        def quant(dst, src, fmt):
+            nc.vector.quantize_mx(out=dst[0][:].bitcast(fmt), scales=dst[1][:], in_=src[:])
+
+        def q_a(g, c):
+            quant(tok_major[(g, c)], st_a[(g, c)], E5)
+
+        def q_b(g, c, pair):
+            quant(feat_major[(g, c, pair)], st_b[(g, c, pair)], E5)
+
+        def q_w(c, h):
+            quant(w_mx[(c, h)], st_w[(c, h)], E4)
+
+        def q_x(g, h):
+            quant(x_mx[(g, h)], st_a[("x", g, h)], E4)
+
+        def passes_into(bank, passes, lfmt, rfmt, start, stop):
+            for i, (lhs, col, rhs) in enumerate(passes):
+                nc.tensor.matmul_mx(out=bank[:], lhsT=lhs[0][:, col:col + P].bitcast(lfmt), lhsT_scale=lhs[1][:, col:col + P],
+                                    rhs=rhs[0][:].bitcast(rfmt), rhs_scale=rhs[1][:],
+                                    start=(start and i == 0), stop=(stop and i == len(passes) - 1))
+
+        dw_dst = {QA: out_1[:, 0:512], QB: out_1[:, 512:1024], KK: out_2, VV: out_3}
+        sums = {}
+
+        def dw_mm(c, d2):
+            for a in range(2):
+                dt = 2 * d2 + a
+                bank = take_bank(mm_ring)[0]
+                sums[("dw", c, d2, a)] = bank
+                passes_into(bank, [(x_mx[(g, dt // 4)], P * (dt % 4), tok_major[(g, c)]) for g in range(2)], E4, E5, True, True)
+
+        def dx_passes(g, t, h, chunks):
+            return [(feat_major[(g, c, t // 2)], P * (t % 2), w_mx[(c, h)]) for c in chunks]
+
+        def dx_mm(g, t):
+            for h in range(2):
+                bank = take_bank(mm_ring)[0]
+                sums[("dx", g, t, h)] = bank
+                passes_into(bank, dx_passes(g, t, h, (VV, KK, QA, QB)), E5, E4, True, True)
+
+        def empty(key, engs, dst):
+            res = work.tile([P, 1024], F32, name="res", tag="res", bufs=5)
+            for a in range(2):
+                copy(engs[a], res[:, 512 * a:512 * (a + 1)], sums[key + (a,)][:])
+            nc.sync.dma_start(out=dst, in_=res[:].rearrange("p (a n) -> p a n", a=2))
+
+        def dw_out(c, d2, engs="ss"):
+            empty(("dw", c, d2), engs, dw_dst[c][256 * d2:256 * (d2 + 1), :].rearrange("(a p) n -> p a n", p=P))
+
+        def dx_out(g, t, engs="ss"):
+            empty(("dx", g, t), engs,
+                  out_0[0, 512 * g:512 * (g + 1), :].rearrange("(p t) (a n) -> p t a n", t=4, a=2)[:, t, :, :])
+
+        def dw(c, d2, engs="ss"):
+            dw_mm(c, d2)
+            dw_out(c, d2, engs)
+
+        def dx(g, t, engs="ss"):
+            dx_mm(g, t)
+            dx_out(g, t, engs)
+
+        held = {}
+
+        def dx_open(g, t, chunks):
+            for h in range(2):
+                first = (g, t, h) not in held
+                if first:
+                    sums[("dx", g, t, h)], held[(g, t, h)] = take_bank(mm_ring, hold=True)
+                passes_into(sums[("dx", g, t, h)], dx_passes(g, t, h, chunks), E5, E4, first, False)
+
+        def dx_close(g, t, chunks, engs="ss"):
+            for h in range(2):
+                passes_into(sums[("dx", g, t, h)], dx_passes(g, t, h, chunks), E5, E4, False, True)
+                mm_ring.append(held[(g, t, h)])
+            dx_out(g, t, engs)
+
+        load_g(0, KK)
+        load_x(0)
+        load_g(0, QA)
+        load_v(0)
+        load_x(1)
+        load_v(1)
+        load_wv()
+        load_g(0, QB)
+        load_wk()
+        load_wq(0)
+        load_wq(1)
+        load_g(1, KK)
+        tables()
+        weave_x("s", 0, 0)
+        mult(0, KK, 0)
+        mult(0, KK, 1)
+        mult(0, KK, 2)
+        add(0, KK, 0)
+        weave_x("s", 0, 1)
+        turn_dz(0, KK, 0)
+        mult(0, KK, 3)
+        q_x(0, 0)
+        add(0, KK, 1)
+        load_g(1, QA)
+        weave_x("s", 1, 0)
+        weave_dz("v", 0, VV)
+        q_x(0, 1)
+        weave_x("s", 1, 1)
+        turn_dz(0, KK, 1)
+        turn_dz(0, VV, 0)
+        turn_w(VV, 0)
+        turn_w(VV, 1)
+        mult(0, QA, 0)
+        q_a(0, VV)
+        q_b(0, KK, 0)
+        mult(0, QA, 1)
+        q_x(1, 0)
+        add(0, QA, 0)
+        weave_dz("v", 1, VV)
+        q_x(1, 1)
+        turn_dz(0, QA, 0)
+        turn_w(KK, 0)
+        mult(0, QB, 0)
+        q_a(1, VV)
+        q_w(VV, 0)
+        turn_w(KK, 1)
+        dw_mm(VV, 0)
+        dw_mm(VV, 1)
+        q_b(0, KK, 1)
+        q_b(0, VV, 0)
+        mult(0, QB, 1)
+        q_w(VV, 1)
+        turn_w(QA, 0)
+        q_w(KK, 0)
+        turn_w(QB, 0)
+        add(0, QB, 0)
+        turn_dz(0, QB, 0)
+        q_w(KK, 1)
+        turn_w(QA, 1)
+        mult(0, QA, 2)
+        q_b(0, QA, 0)
+        q_w(QA, 0)
+        turn_w(QB, 1)
+        dw_out(VV, 0)
+        dw_out(VV, 1)
+        dw_mm(VV, 2)
+        mult(0, QA, 3)
+        load_g(1, QB)
+        q_w(QB, 0)
+        q_b(0, QB, 0)
+        add(0, QA, 1)
+        q_w(QA, 1)
+        turn_dz(0, QA, 1)
+        turn_dz(0, VV, 1)
+        dw_mm(VV, 3)
+        dw_out(VV, 2)
+        mult(0, QB, 2)
+        q_w(QB, 1)
+        dx_mm(0, 0)
+        dw_out(VV, 3)
+        mult(0, QB, 3)
+        q_b(0, QA, 1)
+        q_b(0, VV, 1)
+        add(0, QB, 1)
+        dx_out(0, 0)
+        turn_dz(0, QB, 1)
+        dx(0, 1)
+        weave_dz("s", 0, KK)
+        mult(1, KK, 0)
+        q_b(0, QB, 1)
+        mult(1, KK, 1)
+        dx(0, 2)
+        turn_dz(1, VV, 0)
+        add(1, KK, 0)
+        turn_dz(1, KK, 0)
+        dx(0, 3)
+        turn_dz(1, VV, 1)
+        mult(1, KK, 2)
+        q_a(0, KK)
+        mult(1, KK, 3)
+        q_b(1, VV, 0)
+        add(1, KK, 1)
+        weave_dz("s", 1, KK)
+        turn_dz(1, KK, 1)
+        weave_dz("s", 0, QA)
+        mult(1, QA, 0)
+        q_b(1, VV, 1)
+        q_b(1, KK, 0)
+        mult(1, QA, 1)
+        q_a(1, KK)
+        add(1, QA, 0)
+        dw(KK, 0)
+        dw(KK, 1)
+        turn_dz(1, QA, 0)
+        dw(KK, 2)
+        dw(KK, 3)
+        mult(1, QA, 2)
+        q_b(1, KK, 1)
+        q_a(0, QA)
+        dx_open(1, 3, [VV, KK])
+        mult(1, QA, 3)
+        q_b(1, QA, 0)
+        add(1, QA, 1)
+        turn_dz(1, QA, 1)
+        weave_dz("s", 0, QB)
+        weave_dz("v", 1, QA)
+        mult(1, QB, 0)
+        q_a(1, QA)
+        dw(QA, 0)
+        dw(QA, 1)
+        mult(1, QB, 1)
+        q_b(1, QA, 1)
+        add(1, QB, 0)
+        q_a(0, QB)
+        dw_mm(QA, 2)
+        turn_dz(1, QB, 0)
+        dw_out(QA, 2)
+        dw(QA, 3)
+        mult(1, QB, 2)
+        q_b(1, QB, 0)
+        dx_open(1, 3, [QA])
+        dx(1, 0)
+        mult(1, QB, 3)
+        add(1, QB, 1)
+        turn_dz(1, QB, 1)
+        dx_mm(1, 1)
+        dx_out(1, 1)
+        weave_dz("v", 1, QB)
+        q_b(1, QB, 1)
+        q_a(1, QB)
+        dx_close(1, 3, [QB], "vs")
+        dw(QB, 0, "vs")
+        dw(QB, 1, "vs")
+        dx(1, 2, "vs")
+        dw(QB, 2, "vs")
+        dw(QB, 3, "vs")

@@ -50,10 +50,11 @@ def tile_ringattention_pa_v_kernel(tc, hidden_states, Wq, Wk, Wv, grad_0, grad_1
                                   in_=grad_2[0, h, 512 * g:512 * (g + 1), :].rearrange("(p t) d -> p t d", t=4))
             nat[(g, VV)] = tl
 
-        def load_x(g):
-            tl = keep.tile([P, 4096], BF16, name="raw_x%d" % g)
-            nc.sync.dma_start(out=tl[:], in_=hidden_states[0, 512 * g:512 * (g + 1), :].rearrange("(p t) d -> p (t d)", t=4))
-            raw_x[g] = tl
+        def load_xh(g, h):
+            tl = keep.tile([P, 2048], BF16, name="raw_x%d%d" % (g, h))
+            nc.sync.dma_start(out=tl[:].rearrange("p (t d) -> p t d", t=4),
+                              in_=hidden_states[0, 512 * g:512 * (g + 1), 512 * h:512 * (h + 1)].rearrange("(p t) d -> p t d", t=4))
+            raw_x[(g, h)] = tl
 
         def load_w(src, name, rows, chunks):
             n = (rows.stop - rows.start) // P
@@ -109,7 +110,8 @@ def tile_ringattention_pa_v_kernel(tc, hidden_states, Wq, Wk, Wv, grad_0, grad_1
                 nc.scalar.activation(out=table[g][:, :, 1, :], in_=r.rearrange("p (t j) -> p t j", t=4), func=ACT.Sin,
                                      scale=2 * math.pi)
 
-        turn_ring, mm_ring = [0, 1], [2, 3, 4, 5, 6, 7]
+        mm_ring = [0, 1, 2, 3, 4, 5, 6, 7]
+        turn_ring = mm_ring
 
         def take_bank(ring, hold=False):
             b = ring[0]
@@ -164,7 +166,7 @@ def tile_ringattention_pa_v_kernel(tc, hidden_states, Wq, Wk, Wv, grad_0, grad_1
                            in_=bank[:].rearrange("p (a u r) -> p a r u", a=2, u=2))
 
         def turn_dz(g, c, pair):
-            tl = work.tile([P, 1024], BF16, name="st_b", tag="st_b", bufs=4, align_bytes=64)
+            tl = work.tile([P, 1024], BF16, name="st_b", tag="st_b", bufs=5, align_bytes=64)
             st_b[(g, c, pair)] = tl
             turn([nat[(g, c)][:, 512 * t:512 * (t + 1)] for t in (2 * pair, 2 * pair + 1)], tl[:])
 
@@ -183,7 +185,7 @@ def tile_ringattention_pa_v_kernel(tc, hidden_states, Wq, Wk, Wv, grad_0, grad_1
             weave(eng, (g, c), nat[(g, c)][:].rearrange("p (t f) -> p t f", t=4))
 
         def weave_x(eng, g, h):
-            weave(eng, ("x", g, h), raw_x[g][:].rearrange("p (t f) -> p t f", t=4)[:, :, 512 * h:512 * (h + 1)])
+            weave(eng, ("x", g, h), raw_x[(g, h)][:].rearrange("p (t f) -> p t f", t=4))
 
         def quant(dst, src, fmt):
             nc.vector.quantize_mx(out=dst[0][:].bitcast(fmt), scales=dst[1][:], in_=src[:])
@@ -246,6 +248,23 @@ def tile_ringattention_pa_v_kernel(tc, hidden_states, Wq, Wk, Wv, grad_0, grad_1
             dx_mm(g, t)
             dx_out(g, t, engs)
 
+        results = {}
+
+        def dw1(c, dt):
+            bank = take_bank(mm_ring)[0]
+            sums[("dw", c, dt // 2, dt % 2)] = bank
+            passes_into(bank, [(x_mx[(g, dt // 4)], P * (dt % 4), tok_major[(g, c)]) for g in range(2)], E4, E5, True, True)
+
+        def cp(kind, c, dt):
+            d2, a = dt // 2, dt % 2
+            if a == 0:
+                results[(c, d2)] = work.tile([P, 1024], F32, name="res", tag="res", bufs=5)
+            res = results[(c, d2)]
+            copy("s", res[:, 512 * a:512 * (a + 1)], sums[(kind, c, d2, a)][:])
+            if a == 1:
+                nc.sync.dma_start(out=dw_dst[c][256 * d2:256 * (d2 + 1), :].rearrange("(a p) n -> p a n", p=P),
+                                  in_=res[:].rearrange("p (a n) -> p a n", a=2))
+
         held = {}
 
         def dx_open(g, t, chunks):
@@ -262,158 +281,169 @@ def tile_ringattention_pa_v_kernel(tc, hidden_states, Wq, Wk, Wv, grad_0, grad_1
             dx_out(g, t, engs)
 
         load_g(0, KK)
-        load_x(0)
-        load_g(0, QA)
+        load_xh(0, 0)
+        load_xh(1, 0)
         load_v(0)
-        load_x(1)
         load_v(1)
-        load_wv()
-        load_g(0, QB)
-        load_wk()
-        load_wq(0)
-        load_wq(1)
         load_g(1, KK)
+        load_xh(0, 1)
+        load_xh(1, 1)
+        load_wv()
+        load_wk()
+        load_g(0, QA)
+        load_wq(0)
+        load_g(0, QB)
+        load_wq(1)
         tables()
         weave_x("s", 0, 0)
+        weave_x("s", 1, 0)
         mult(0, KK, 0)
         mult(0, KK, 1)
         mult(0, KK, 2)
         add(0, KK, 0)
-        weave_x("s", 0, 1)
-        turn_dz(0, KK, 0)
-        mult(0, KK, 3)
         q_x(0, 0)
-        add(0, KK, 1)
-        load_g(1, QA)
-        weave_x("s", 1, 0)
         weave_dz("v", 0, VV)
-        q_x(0, 1)
-        weave_x("s", 1, 1)
-        turn_dz(0, KK, 1)
-        turn_dz(0, VV, 0)
-        turn_w(VV, 0)
-        turn_w(VV, 1)
-        mult(0, QA, 0)
-        q_a(0, VV)
-        q_b(0, KK, 0)
-        mult(0, QA, 1)
+        weave_dz("s", 1, VV)
+        mult(0, KK, 3)
+        load_g(1, QA)
         q_x(1, 0)
-        add(0, QA, 0)
-        weave_dz("v", 1, VV)
-        q_x(1, 1)
-        turn_dz(0, QA, 0)
-        turn_w(KK, 0)
-        mult(0, QB, 0)
+        q_a(0, VV)
+        weave_x("s", 0, 1)
+        add(0, KK, 1)
         q_a(1, VV)
+        weave_x("s", 1, 1)
+        for i in range(4):
+            dw1(VV, i)
+        mult(1, KK, 0)
+        mult(1, KK, 1)
+        q_x(0, 1)
+        weave_dz("s", 0, KK)
+        add(1, KK, 0)
+        turn_w(VV, 0)
+        cp("dw", VV, 0)
+        cp("dw", VV, 1)
+        mult(1, KK, 2)
+        q_x(1, 1)
+        dw1(VV, 4)
+        turn_w(VV, 1)
+        cp("dw", VV, 2)
+        cp("dw", VV, 3)
+        dw1(VV, 5)
+        mult(1, KK, 3)
+        load_g(1, QB)
         q_w(VV, 0)
-        turn_w(KK, 1)
-        dw_mm(VV, 0)
-        dw_mm(VV, 1)
-        q_b(0, KK, 1)
-        q_b(0, VV, 0)
-        mult(0, QB, 1)
+        add(1, KK, 1)
+        turn_w(KK, 0)
+        cp("dw", VV, 4)
+        cp("dw", VV, 5)
+        dw1(VV, 6)
+        q_a(0, KK)
+        weave_dz("v", 1, KK)
         q_w(VV, 1)
-        turn_w(QA, 0)
+        q_a(1, KK)
+        turn_w(KK, 1)
+        dw1(VV, 7)
+        mult(0, QA, 0)
         q_w(KK, 0)
-        turn_w(QB, 0)
-        add(0, QB, 0)
-        turn_dz(0, QB, 0)
+        turn_dz(0, KK, 0)
+        turn_dz(0, VV, 0)
+        cp("dw", VV, 6)
+        cp("dw", VV, 7)
+        dw_mm(KK, 0)
+        turn_w(QA, 0)
+        dw_out(KK, 0)
+        mult(0, QA, 1)
         q_w(KK, 1)
+        add(0, QA, 0)
+        q_b(0, KK, 0)
+        q_b(0, VV, 0)
+        dw_mm(KK, 1)
+        turn_w(QB, 0)
+        dw_out(KK, 1)
+        mult(0, QB, 0)
+        q_w(QA, 0)
+        dw_mm(KK, 2)
         turn_w(QA, 1)
+        turn_dz(0, QA, 0)
+        dw_out(KK, 2)
+        mult(0, QB, 1)
+        q_w(QB, 0)
+        add(0, QB, 0)
+        dw_mm(KK, 3)
+        turn_w(QB, 1)
+        turn_dz(0, QB, 0)
+        dw_out(KK, 3)
+        turn_dz(0, KK, 1)
+        turn_dz(0, VV, 1)
         mult(0, QA, 2)
         q_b(0, QA, 0)
-        q_w(QA, 0)
-        turn_w(QB, 1)
-        dw_out(VV, 0)
-        dw_out(VV, 1)
-        dw_mm(VV, 2)
-        mult(0, QA, 3)
-        load_g(1, QB)
-        q_w(QB, 0)
-        q_b(0, QB, 0)
-        add(0, QA, 1)
         q_w(QA, 1)
-        turn_dz(0, QA, 1)
-        turn_dz(0, VV, 1)
-        dw_mm(VV, 3)
-        dw_out(VV, 2)
-        mult(0, QB, 2)
+        mult(0, QA, 3)
+        q_b(0, QB, 0)
         q_w(QB, 1)
-        dx_mm(0, 0)
-        dw_out(VV, 3)
+        add(0, QA, 1)
+        dx(0, 0)
+        turn_dz(0, QA, 1)
+        dx(0, 1)
+        turn_dz(1, KK, 0)
+        turn_dz(1, VV, 0)
+        mult(0, QB, 2)
+        q_b(0, KK, 1)
+        q_b(0, VV, 1)
         mult(0, QB, 3)
         q_b(0, QA, 1)
-        q_b(0, VV, 1)
         add(0, QB, 1)
-        dx_out(0, 0)
         turn_dz(0, QB, 1)
-        dx(0, 1)
-        weave_dz("s", 0, KK)
-        mult(1, KK, 0)
-        q_b(0, QB, 1)
-        mult(1, KK, 1)
-        dx(0, 2)
-        turn_dz(1, VV, 0)
-        add(1, KK, 0)
-        turn_dz(1, KK, 0)
-        dx(0, 3)
-        turn_dz(1, VV, 1)
-        mult(1, KK, 2)
-        q_a(0, KK)
-        mult(1, KK, 3)
-        q_b(1, VV, 0)
-        add(1, KK, 1)
-        weave_dz("s", 1, KK)
-        turn_dz(1, KK, 1)
         weave_dz("s", 0, QA)
         mult(1, QA, 0)
-        q_b(1, VV, 1)
+        q_b(0, QB, 1)
+        dx(0, 2)
+        dx(0, 3)
         q_b(1, KK, 0)
         mult(1, QA, 1)
-        q_a(1, KK)
+        q_b(1, VV, 0)
         add(1, QA, 0)
-        dw(KK, 0)
-        dw(KK, 1)
         turn_dz(1, QA, 0)
-        dw(KK, 2)
-        dw(KK, 3)
+        turn_dz(1, KK, 1)
+        turn_dz(1, VV, 1)
+        weave_dz("s", 0, QB)
+        dx_open(1, 0, [VV, KK])
+        dx_open(1, 1, [VV, KK])
         mult(1, QA, 2)
-        q_b(1, KK, 1)
         q_a(0, QA)
-        dx_open(1, 3, [VV, KK])
         mult(1, QA, 3)
         q_b(1, QA, 0)
+        dx_open(1, 0, [QA])
+        dx_open(1, 1, [QA])
         add(1, QA, 1)
         turn_dz(1, QA, 1)
-        weave_dz("s", 0, QB)
+        q_b(1, KK, 1)
         weave_dz("v", 1, QA)
-        mult(1, QB, 0)
+        q_b(1, VV, 1)
         q_a(1, QA)
         dw(QA, 0)
         dw(QA, 1)
+        dw(QA, 2)
+        mult(1, QB, 0)
         mult(1, QB, 1)
         q_b(1, QA, 1)
         add(1, QB, 0)
-        q_a(0, QB)
-        dw_mm(QA, 2)
         turn_dz(1, QB, 0)
-        dw_out(QA, 2)
         dw(QA, 3)
         mult(1, QB, 2)
         q_b(1, QB, 0)
-        dx_open(1, 3, [QA])
-        dx(1, 0)
+        dx_close(1, 0, [QB])
+        dx_close(1, 1, [QB])
+        dx_open(1, 2, [VV, KK, QA])
         mult(1, QB, 3)
+        q_a(0, QB)
         add(1, QB, 1)
         turn_dz(1, QB, 1)
-        dx_mm(1, 1)
-        dx_out(1, 1)
+        dx_open(1, 3, [VV, KK, QA])
         weave_dz("v", 1, QB)
         q_b(1, QB, 1)
         q_a(1, QB)
+        dx_close(1, 2, [QB], "vs")
         dx_close(1, 3, [QB], "vs")
-        dw(QB, 0, "vs")
-        dw(QB, 1, "vs")
-        dx(1, 2, "vs")
-        dw(QB, 2, "vs")
-        dw(QB, 3, "vs")
+        for d2 in range(4):
+            dw(QB, d2, "vs")

@@ -50,6 +50,14 @@ def tile_ringattention_pa_v_kernel(tc, hidden_states, Wq, Wk, Wv, grad_0, grad_1
                                   in_=grad_2[0, h, 512 * g:512 * (g + 1), :].rearrange("(p t) d -> p t d", t=4))
             nat[(g, VV)] = tl
 
+        def load_x(g):
+            tl = keep.tile([P, 4096], BF16, name="raw_x%d" % g)
+            nc.sync.dma_start(out=tl[:], in_=hidden_states[0, 512 * g:512 * (g + 1), :].rearrange("(p t) d -> p (t d)", t=4))
+            raw_x[g] = tl
+
+        def load_vraw(g):
+            load_g(g, VV)
+
         def load_xh(g, h):
             tl = keep.tile([P, 2048], BF16, name="raw_x%d%d" % (g, h))
             nc.sync.dma_start(out=tl[:].rearrange("p (t d) -> p t d", t=4),
@@ -143,7 +151,7 @@ def tile_ringattention_pa_v_kernel(tc, hidden_states, Wq, Wk, Wv, grad_0, grad_1
             tl = prod[(g, c, t // 2)]
             gr = raw_g[(g, c)][:].rearrange("p (h t d) -> p t h d", h=4, t=4)[:, t, :, :]
             nc.vector.tensor_tensor(
-                out=tl[:, 1024 * (t % 2):1024 * (t % 2 + 1)].rearrange("p (s h d) -> p s h d", s=2, h=4),
+                out=tl[:].rearrange("p (f t h d) -> p t f h d", f=2, t=2, h=4)[:, t % 2, :, :, :],
                 in0=gr.unsqueeze(1).to_broadcast([P, 2, 4, HD]),
                 in1=table[g][:, t, :, :].unsqueeze(2).to_broadcast([P, 2, 8, HALF]),
                 op=ALU.mult)
@@ -151,41 +159,53 @@ def tile_ringattention_pa_v_kernel(tc, hidden_states, Wq, Wk, Wv, grad_0, grad_1
         def add(g, c, pair):
             if pair == 0:
                 nat[(g, c)] = work.tile([P, 2048], BF16, name="nat", tag="nat", bufs=4, align_bytes=64)
-            dst = nat[(g, c)][:, 1024 * pair:1024 * (pair + 1)].rearrange("p (t h s j) -> p t h s j", t=2, h=4, s=2)
-            m = prod[(g, c, pair)][:].rearrange("p (t f h s j) -> p t f h s j", t=2, f=2, h=4, s=2)
-            nc.vector.tensor_tensor(out=dst[:, :, :, 0, :], in0=m[:, :, 0, :, 0, :], in1=m[:, :, 1, :, 1, :], op=ALU.add)
-            nc.vector.tensor_tensor(out=dst[:, :, :, 1, :], in0=m[:, :, 0, :, 1, :], in1=m[:, :, 1, :, 0, :], op=ALU.subtract)
+            m = prod[(g, c, pair)][:].rearrange("p (f k s q u e) -> p f s u k q e", f=2, s=2, q=16, u=2, e=2)
+            for u in range(2):
+                dst = nat[(g, c)][:, 1024 * u + 512 * pair:1024 * u + 512 * (pair + 1)].rearrange(
+                    "p (k s q e) -> p s k q e", s=2, q=16, e=2)
+                nc.vector.tensor_tensor(out=dst[:, 0, :, :, :], in0=m[:, 0, 0, u, :, :, :], in1=m[:, 1, 1, u, :, :, :], op=ALU.add)
+                nc.vector.tensor_tensor(out=dst[:, 1, :, :, :], in0=m[:, 0, 1, u, :, :, :], in1=m[:, 1, 0, u, :, :, :], op=ALU.subtract)
+
+        def halves(row):
+            words = row.bitcast(F32)
+            return [words[:, u:256:2] for u in range(2)]
 
         def turn(srcs, dst):
             bank = take_bank(turn_ring)[0]
             for a in range(2):
-                words = srcs[a].bitcast(F32)
                 for u in range(2):
-                    nc.tensor.transpose(bank[:, 256 * a + 128 * u:256 * a + 128 * (u + 1)], words[:, u:256:2], ident[:])
+                    nc.tensor.transpose(bank[:, 256 * a + 128 * u:256 * a + 128 * (u + 1)], srcs[a][u], ident[:])
             nc.scalar.copy(out=dst.bitcast(F32).rearrange("p (a r u) -> p a r u", a=2, u=2),
                            in_=bank[:].rearrange("p (a u r) -> p a r u", a=2, u=2))
 
         def turn_dz(g, c, pair):
             tl = work.tile([P, 1024], BF16, name="st_b", tag="st_b", bufs=5, align_bytes=64)
             st_b[(g, c, pair)] = tl
-            turn([nat[(g, c)][:, 512 * t:512 * (t + 1)] for t in (2 * pair, 2 * pair + 1)], tl[:])
+            if c == VV:
+                turn([halves(nat[(g, c)][:, 512 * t:512 * (t + 1)]) for t in (2 * pair, 2 * pair + 1)], tl[:])
+            else:
+                turn([[nat[(g, c)][:, 1024 * u + 256 * t:1024 * u + 256 * (t + 1)].bitcast(F32) for u in range(2)]
+                      for t in (2 * pair, 2 * pair + 1)], tl[:])
 
         def turn_w(c, h):
             tl = work.tile([P, 2048], BF16, name="st_w", tag="st_w", bufs=3, align_bytes=64)
             st_w[(c, h)] = tl
             for b in range(2):
-                turn([raw_w[(c, 4 * h + 2 * b + a)] for a in range(2)], tl[:, 1024 * b:1024 * (b + 1)])
+                turn([halves(raw_w[(c, 4 * h + 2 * b + a)]) for a in range(2)], tl[:, 1024 * b:1024 * (b + 1)])
 
-        def weave(eng, key, src):
+        def weave(eng, key, src, order, **sizes):
             tl = work.tile([P, 2048], BF16, name="st_a", tag="st_a", bufs=3, align_bytes=64)
             st_a[key] = tl
-            copy(eng, tl[:].rearrange("p (c i t) -> p c t i", i=4, t=4), src.rearrange("p t (c i) -> p c t i", i=4))
+            copy(eng, tl[:].rearrange(order, i=4, t=4, **sizes), src)
 
         def weave_dz(eng, g, c):
-            weave(eng, (g, c), nat[(g, c)][:].rearrange("p (t f) -> p t f", t=4))
+            weave(eng, (g, c), nat[(g, c)][:].rearrange("p (u t c i) -> p u c t i", u=2, t=4, i=4), "p (u c i t) -> p u c t i", u=2)
+
+        def weave_v(eng, g):
+            weave(eng, (g, VV), raw_g[(g, VV)][:].rearrange("p (h t c i) -> p h c t i", h=4, t=4, i=4), "p (h c i t) -> p h c t i", h=4)
 
         def weave_x(eng, g, h):
-            weave(eng, ("x", g, h), raw_x[(g, h)][:].rearrange("p (t f) -> p t f", t=4))
+            weave(eng, ("x", g, h), raw_x[g][:].rearrange("p (t f) -> p t f", t=4)[:, :, 512 * h:512 * (h + 1)].rearrange("p t (c i) -> p c t i", i=4), "p (c i t) -> p c t i")
 
         def quant(dst, src, fmt):
             nc.vector.quantize_mx(out=dst[0][:].bitcast(fmt), scales=dst[1][:], in_=src[:])
@@ -230,7 +250,11 @@ def tile_ringattention_pa_v_kernel(tc, hidden_states, Wq, Wk, Wv, grad_0, grad_1
         def empty(key, engs, dst):
             res = work.tile([P, 1024], F32, name="res", tag="res", bufs=5)
             for a in range(2):
-                copy(engs[a], res[:, 512 * a:512 * (a + 1)], sums[key + (a,)][:])
+                if key[0] == "dw" and key[1] != VV:
+                    copy(engs[a], res[:, 512 * a:512 * (a + 1)].rearrange("p (m u e) -> p m u e", u=2, e=2),
+                         sums[key + (a,)][:].rearrange("p (u m e) -> p m u e", u=2, e=2))
+                else:
+                    copy(engs[a], res[:, 512 * a:512 * (a + 1)], sums[key + (a,)][:])
             nc.sync.dma_start(out=dst, in_=res[:].rearrange("p (a n) -> p a n", a=2))
 
         def dw_out(c, d2, engs="ss"):
@@ -281,126 +305,129 @@ def tile_ringattention_pa_v_kernel(tc, hidden_states, Wq, Wk, Wv, grad_0, grad_1
             dx_out(g, t, engs)
 
         load_g(0, KK)
-        load_xh(0, 0)
-        load_xh(1, 0)
-        load_v(0)
-        load_v(1)
+        load_x(0)
+        load_vraw(0)
+        load_x(1)
+        load_vraw(1)
         load_g(1, KK)
-        load_xh(0, 1)
-        load_xh(1, 1)
         load_wv()
-        load_wk()
-        load_g(0, QA)
-        load_wq(0)
-        load_g(0, QB)
-        load_wq(1)
         tables()
         weave_x("s", 0, 0)
-        weave_x("s", 1, 0)
+        weave_x("s", 0, 1)
         mult(0, KK, 0)
         mult(0, KK, 1)
         mult(0, KK, 2)
         add(0, KK, 0)
-        q_x(0, 0)
-        weave_dz("v", 0, VV)
-        weave_dz("s", 1, VV)
         mult(0, KK, 3)
-        load_g(1, QA)
-        q_x(1, 0)
-        q_a(0, VV)
-        weave_x("s", 0, 1)
-        add(0, KK, 1)
-        q_a(1, VV)
-        weave_x("s", 1, 1)
-        for i in range(4):
-            dw1(VV, i)
-        mult(1, KK, 0)
-        mult(1, KK, 1)
+        load_wk()
+        load_g(0, QA)
+        load_wq(0)
+        q_x(0, 0)
+        weave_x("s", 1, 0)
+        weave_v("v", 0)
+        load_g(0, QB)
+        load_wq(1)
+        load_v(0)
         q_x(0, 1)
-        weave_dz("s", 0, KK)
-        add(1, KK, 0)
+        weave_v("s", 1)
+        load_g(1, QA)
+        q_a(0, VV)
+        add(0, KK, 1)
+        q_x(1, 0)
+        weave_x("s", 1, 1)
+        mult(1, KK, 0)
+        q_a(1, VV)
         turn_w(VV, 0)
+        dw1(VV, 0)
+        dw1(VV, 1)
+        weave_dz("s", 0, KK)
+        mult(1, KK, 1)
+        q_x(1, 1)
+        add(1, KK, 0)
+        turn_w(VV, 1)
+        dw1(VV, 2)
         cp("dw", VV, 0)
         cp("dw", VV, 1)
+        dw1(VV, 3)
         mult(1, KK, 2)
-        q_x(1, 1)
-        dw1(VV, 4)
-        turn_w(VV, 1)
-        cp("dw", VV, 2)
-        cp("dw", VV, 3)
-        dw1(VV, 5)
+        q_w(VV, 0)
         mult(1, KK, 3)
         load_g(1, QB)
-        q_w(VV, 0)
-        add(1, KK, 1)
+        load_v(1)
+        q_a(0, KK)
         turn_w(KK, 0)
+        cp("dw", VV, 2)
+        cp("dw", VV, 3)
+        dw1(VV, 4)
+        dw1(VV, 5)
+        add(1, KK, 1)
+        q_w(VV, 1)
+        weave_dz("v", 1, KK)
+        turn_w(KK, 1)
         cp("dw", VV, 4)
         cp("dw", VV, 5)
         dw1(VV, 6)
-        q_a(0, KK)
-        weave_dz("v", 1, KK)
-        q_w(VV, 1)
-        q_a(1, KK)
-        turn_w(KK, 1)
         dw1(VV, 7)
-        mult(0, QA, 0)
         q_w(KK, 0)
-        turn_dz(0, KK, 0)
-        turn_dz(0, VV, 0)
+        q_a(1, KK)
+        mult(0, QA, 0)
+        turn_w(QA, 0)
         cp("dw", VV, 6)
         cp("dw", VV, 7)
         dw_mm(KK, 0)
-        turn_w(QA, 0)
-        dw_out(KK, 0)
+        turn_dz(0, KK, 0)
+        turn_dz(0, KK, 1)
         mult(0, QA, 1)
         q_w(KK, 1)
         add(0, QA, 0)
-        q_b(0, KK, 0)
-        q_b(0, VV, 0)
-        dw_mm(KK, 1)
+        dw_out(KK, 0)
         turn_w(QB, 0)
-        dw_out(KK, 1)
-        mult(0, QB, 0)
+        dw_mm(KK, 1)
         q_w(QA, 0)
-        dw_mm(KK, 2)
+        mult(0, QB, 0)
+        q_b(0, KK, 0)
+        q_b(0, KK, 1)
         turn_w(QA, 1)
-        turn_dz(0, QA, 0)
-        dw_out(KK, 2)
+        dw_out(KK, 1)
+        dw_mm(KK, 2)
         mult(0, QB, 1)
         q_w(QB, 0)
-        add(0, QB, 0)
-        dw_mm(KK, 3)
+        turn_dz(0, QA, 0)
+        turn_dz(0, VV, 0)
         turn_w(QB, 1)
+        dw_out(KK, 2)
+        add(0, QB, 0)
         turn_dz(0, QB, 0)
-        dw_out(KK, 3)
-        turn_dz(0, KK, 1)
+        dw_mm(KK, 3)
         turn_dz(0, VV, 1)
+        q_w(QA, 1)
         mult(0, QA, 2)
         q_b(0, QA, 0)
-        q_w(QA, 1)
+        q_b(0, VV, 0)
         mult(0, QA, 3)
-        q_b(0, QB, 0)
         q_w(QB, 1)
+        q_b(0, QB, 0)
         add(0, QA, 1)
-        dx(0, 0)
+        dw_out(KK, 3)
+        dx_mm(0, 0)
         turn_dz(0, QA, 1)
+        dx_out(0, 0)
         dx(0, 1)
-        turn_dz(1, KK, 0)
-        turn_dz(1, VV, 0)
         mult(0, QB, 2)
-        q_b(0, KK, 1)
         q_b(0, VV, 1)
         mult(0, QB, 3)
         q_b(0, QA, 1)
         add(0, QB, 1)
         turn_dz(0, QB, 1)
+        turn_dz(1, KK, 0)
+        turn_dz(1, VV, 0)
         weave_dz("s", 0, QA)
         mult(1, QA, 0)
         q_b(0, QB, 1)
         dx(0, 2)
         dx(0, 3)
-        q_b(1, KK, 0)
         mult(1, QA, 1)
+        q_b(1, KK, 0)
         q_b(1, VV, 0)
         add(1, QA, 0)
         turn_dz(1, QA, 0)

import math
from contextlib import ExitStack

import concourse.mybir as mybir
from concourse.masks import make_identity

S, D, HD = 1024, 1024, 128
J = 2048
HALF = HD // 2
THETA = 10000.0
FLOPS = 2 * 2 * S * D * J

F32 = mybir.dt.float32
BF16 = mybir.dt.bfloat16
I32 = mybir.dt.int32
U32 = mybir.dt.uint32
U8 = mybir.dt.uint8
E4 = mybir.dt.float8_e4m3fn_x4
E5 = mybir.dt.float8_e5m2_x4
ALU = mybir.AluOpType
ACT = mybir.ActivationFunctionType

P = 128
QA, QB, KK, VV = 0, 1, 2, 3


def tile_ringattention_pa_v_kernel(tc, hidden_states, Wq, Wk, Wv, grad_0, grad_1, grad_2,
                                                out_0, out_1, out_2, out_3):
    nc = tc.nc
    with ExitStack() as ctx:
        keep = ctx.enter_context(tc.tile_pool(name="keep", bufs=1))
        work = ctx.enter_context(tc.tile_pool(name="work", bufs=2))
        psum = ctx.enter_context(tc.psum_pool(name="psum", bufs=1))
        ctx.enter_context(tc.manual_schedule())

        raw_g, raw_x, raw_w, nat = {}, {}, {}, {}
        grads = {QA: (grad_0, 0), QB: (grad_0, 4), KK: (grad_1, 0), VV: (grad_2, 0)}

        def load_g(g, c):
            src, h0 = grads[c]
            tl = work.tile([P, 2048], BF16, name="raw_g", tag="raw_g", bufs=4)
            nc.sync.dma_start(out=tl[:].rearrange("p (h w) -> p h w", h=4),
                              in_=src[0, h0:h0 + 4, 512 * g:512 * (g + 1), :].rearrange("h (p t) d -> p h (t d)", t=4))
            raw_g[(g, c)] = tl

        def load_v(g):
            tl = keep.tile([P, 2048], BF16, name="nat_v%d" % g, align_bytes=64)
            for h in range(4):
                nc.sync.dma_start(out=tl[:].rearrange("p (t h d) -> p t h d", t=4, h=4)[:, :, h, :],
                                  in_=grad_2[0, h, 512 * g:512 * (g + 1), :].rearrange("(p t) d -> p t d", t=4))
            nat[(g, VV)] = tl

        def load_x(g):
            tl = keep.tile([P, 4096], BF16, name="raw_x%d" % g)
            nc.sync.dma_start(out=tl[:], in_=hidden_states[0, 512 * g:512 * (g + 1), :].rearrange("(p t) d -> p (t d)", t=4))
            raw_x[g] = tl

        def load_vraw(g):
            load_g(g, VV)

        def load_xh(g, h):
            tl = keep.tile([P, 2048], BF16, name="raw_x%d%d" % (g, h))
            nc.sync.dma_start(out=tl[:].rearrange("p (t d) -> p t d", t=4),
                              in_=hidden_states[0, 512 * g:512 * (g + 1), 512 * h:512 * (h + 1)].rearrange("(p t) d -> p t d", t=4))
            raw_x[(g, h)] = tl

        def load_w(src, name, rows, chunks):
            n = (rows.stop - rows.start) // P
            width = 512 * len(chunks)
            tl = keep.tile([P, n * width], BF16, name=name)
            nc.sync.dma_start(out=tl[:].rearrange("p (a w) -> p a w", a=n),
                              in_=src[rows, :].rearrange("(a p) w -> p a w", p=P))
            for a in range(n):
                for i, c in enumerate(chunks):
                    raw_w[(c, rows.start // P + a)] = tl[:, a * width + 512 * i:a * width + 512 * (i + 1)]

        def load_wv():
            load_w(Wv, "raw_wv", slice(0, D), [VV])

        def load_wk():
            load_w(Wk, "raw_wk", slice(0, D), [KK])

        def load_wq(h):
            load_w(Wq, "raw_wq%d" % h, slice(512 * h, 512 * (h + 1)), [QA, QB])

        ident = keep.tile([P, P], F32)
        table = [keep.tile([P, 4, 2, HALF], F32, name="table%d" % g) for g in range(2)]

        def tables():
            ones = keep.tile([P, 8], F32)
            nc.vector.memset(ones[:], 1.0)
            warm = keep.tile([P, 1], F32)
            nc.scalar.activation(out=warm[:], in_=ones[:, 0:1], func=ACT.Sin)
            tok = keep.tile([P, 8], F32)
            nc.gpsimd.iota(tok[:], pattern=[[512, 2], [1, 4]], base=0, channel_multiplier=4, allow_small_or_imprecise_dtypes=True)
            make_identity(nc, ident[:])
            freq = keep.tile([P, HALF], F32)
            for b in range(8):
                nc.vector.tensor_scalar(out=freq[:, b:b + 1], in0=ones[:, b:b + 1], scalar1=THETA ** (-b / HALF) / (2 * math.pi),
                                        scalar2=None, op0=ALU.mult)
            for a in range(1, 8):
                nc.vector.tensor_scalar(out=freq[:, 8 * a:8 * a + 8], in0=freq[:, 0:8], scalar1=THETA ** (-8 * a / HALF),
                                        scalar2=None, op0=ALU.mult)
            whole = work.tile([P, 1024], I32, name="whole", tag="res", bufs=5)
            frac = work.tile([P, 1024], F32, name="frac", tag="res", bufs=5)
            for g in range(2):
                for i in range(4 * g, 4 * g + 4):
                    nc.vector.tensor_scalar(out=whole[:, HALF * i:HALF * (i + 1)], in0=freq[:], scalar1=tok[:, i:i + 1],
                                            scalar2=None, op0=ALU.mult)
                for i in range(4 * g, 4 * g + 4):
                    nc.vector.scalar_tensor_tensor(out=frac[:, HALF * i:HALF * (i + 1)], in0=freq[:], scalar=tok[:, i:i + 1],
                                                   in1=whole[:, HALF * i:HALF * (i + 1)], op0=ALU.mult, op1=ALU.subtract)
                r = frac[:, 256 * g:256 * (g + 1)]
                mag = frac[:, 512 + 256 * g:512 + 256 * (g + 1)]
                nc.scalar.activation(out=mag, in_=r, func=ACT.Abs)
                nc.scalar.activation(out=table[g][:, :, 0, :], in_=mag.rearrange("p (t j) -> p t j", t=4), func=ACT.Sin,
                                     scale=-2 * math.pi, bias=math.pi / 2)
                nc.scalar.activation(out=table[g][:, :, 1, :], in_=r.rearrange("p (t j) -> p t j", t=4), func=ACT.Sin,
                                     scale=2 * math.pi)

        mm_ring = [0, 1, 2, 3, 4, 5, 6, 7]
        turn_ring = mm_ring

        def take_bank(ring, hold=False):
            b = ring[0]
            ring.remove(b)
            if not hold:
                ring.append(b)
            return psum.tile([P, 512], F32, name="bank%d" % b, tag="bank%d" % b), b

        def mx_tiles(name, width):
            codes = keep.tile([P, width], U32, name=name + "_c", align_bytes=64)
            scales = keep.tile([P, width], U8, name=name + "_s", align_bytes=64)
            return codes, scales

        tok_major = {(g, c): mx_tiles("a%d%d" % (g, c), 512) for g in range(2) for c in range(4)}
        feat_major = {(g, c, h): mx_tiles("b%d%d%d" % (g, c, h), 256) for g in range(2) for c in range(4) for h in range(2)}
        w_mx = {(c, h): mx_tiles("w%d%d" % (c, h), 512) for c in range(4) for h in range(2)}
        x_mx = {(g, h): mx_tiles("x%d%d" % (g, h), 512) for g in range(2) for h in range(2)}
        prod, st_a, st_b, st_w = {}, {}, {}, {}

        def copy(eng, out, in_):
            if eng == "v":
                nc.vector.tensor_copy(out=out, in_=in_)
            else:
                nc.scalar.copy(out=out, in_=in_)

        def mult(g, c, t):
            if t % 2 == 0:
                prod[(g, c, t // 2)] = work.tile([P, 2048], F32, name="prod", tag="prod", bufs=2)
            tl = prod[(g, c, t // 2)]
            gr = raw_g[(g, c)][:].rearrange("p (h t d) -> p t h d", h=4, t=4)[:, t, :, :]
            nc.vector.tensor_tensor(
                out=tl[:].rearrange("p (f t h d) -> p t f h d", f=2, t=2, h=4)[:, t % 2, :, :, :],
                in0=gr.unsqueeze(1).to_broadcast([P, 2, 4, HD]),
                in1=table[g][:, t, :, :].unsqueeze(2).to_broadcast([P, 2, 8, HALF]),
                op=ALU.mult)

        def add(g, c, pair):
            if pair == 0:
                nat[(g, c)] = work.tile([P, 2048], BF16, name="nat", tag="nat", bufs=4, align_bytes=64)
            m = prod[(g, c, pair)][:].rearrange("p (f k s q u e) -> p f s u k q e", f=2, s=2, q=16, u=2, e=2)
            for u in range(2):
                dst = nat[(g, c)][:, 1024 * u + 512 * pair:1024 * u + 512 * (pair + 1)].rearrange(
                    "p (k s q e) -> p s k q e", s=2, q=16, e=2)
                nc.vector.tensor_tensor(out=dst[:, 0, :, :, :], in0=m[:, 0, 0, u, :, :, :], in1=m[:, 1, 1, u, :, :, :], op=ALU.add)
                nc.vector.tensor_tensor(out=dst[:, 1, :, :, :], in0=m[:, 0, 1, u, :, :, :], in1=m[:, 1, 0, u, :, :, :], op=ALU.subtract)

        def halves(row):
            words = row.bitcast(F32)
            return [words[:, u:256:2] for u in range(2)]

        def turn(srcs, dst):
            bank = take_bank(turn_ring)[0]
            for a in range(2):
                for u in range(2):
                    nc.tensor.transpose(bank[:, 256 * a + 128 * u:256 * a + 128 * (u + 1)], srcs[a][u], ident[:])
            nc.scalar.copy(out=dst.bitcast(F32).rearrange("p (a r u) -> p a r u", a=2, u=2),
                           in_=bank[:].rearrange("p (a u r) -> p a r u", a=2, u=2))

        def turn_dz(g, c, pair):
            tl = work.tile([P, 1024], BF16, name="st_b", tag="st_b", bufs=5, align_bytes=64)
            st_b[(g, c, pair)] = tl
            if c == VV:
                turn([halves(nat[(g, c)][:, 512 * t:512 * (t + 1)]) for t in (2 * pair, 2 * pair + 1)], tl[:])
            else:
                turn([[nat[(g, c)][:, 1024 * u + 256 * t:1024 * u + 256 * (t + 1)].bitcast(F32) for u in range(2)]
                      for t in (2 * pair, 2 * pair + 1)], tl[:])

        def turn_w(c, h):
            tl = work.tile([P, 2048], BF16, name="st_w", tag="st_w", bufs=3, align_bytes=64)
            st_w[(c, h)] = tl
            for b in range(2):
                turn([halves(raw_w[(c, 4 * h + 2 * b + a)]) for a in range(2)], tl[:, 1024 * b:1024 * (b + 1)])

        def weave(eng, key, src, order, **sizes):
            tl = work.tile([P, 2048], BF16, name="st_a", tag="st_a", bufs=3, align_bytes=64)
            st_a[key] = tl
            copy(eng, tl[:].rearrange(order, i=4, t=4, **sizes), src)

        def weave_dz(eng, g, c):
            weave(eng, (g, c), nat[(g, c)][:].rearrange("p (u t c i) -> p u c t i", u=2, t=4, i=4), "p (u c i t) -> p u c t i", u=2)

        def weave_v(eng, g):
            weave(eng, (g, VV), raw_g[(g, VV)][:].rearrange("p (h t c i) -> p h c t i", h=4, t=4, i=4), "p (h c i t) -> p h c t i", h=4)

        def weave_x(eng, g, h):
            weave(eng, ("x", g, h), raw_x[g][:].rearrange("p (t f) -> p t f", t=4)[:, :, 512 * h:512 * (h + 1)].rearrange("p t (c i) -> p c t i", i=4), "p (c i t) -> p c t i")

        def quant(dst, src, fmt):
            nc.vector.quantize_mx(out=dst[0][:].bitcast(fmt), scales=dst[1][:], in_=src[:])

        def q_a(g, c):
            quant(tok_major[(g, c)], st_a[(g, c)], E5)

        def q_b(g, c, pair):
            quant(feat_major[(g, c, pair)], st_b[(g, c, pair)], E5)

        def q_w(c, h):
            quant(w_mx[(c, h)], st_w[(c, h)], E4)

        def q_x(g, h):
            quant(x_mx[(g, h)], st_a[("x", g, h)], E4)

        def passes_into(bank, passes, lfmt, rfmt, start, stop):
            for i, (lhs, col, rhs) in enumerate(passes):
                nc.tensor.matmul_mx(out=bank[:], lhsT=lhs[0][:, col:col + P].bitcast(lfmt), lhsT_scale=lhs[1][:, col:col + P],
                                    rhs=rhs[0][:].bitcast(rfmt), rhs_scale=rhs[1][:],
                                    start=(start and i == 0), stop=(stop and i == len(passes) - 1))

        dw_dst = {QA: out_1[:, 0:512], QB: out_1[:, 512:1024], KK: out_2, VV: out_3}
        sums = {}

        def dw_mm(c, d2):
            for a in range(2):
                dt = 2 * d2 + a
                bank = take_bank(mm_ring)[0]
                sums[("dw", c, d2, a)] = bank
                passes_into(bank, [(x_mx[(g, dt // 4)], P * (dt % 4), tok_major[(g, c)]) for g in range(2)], E4, E5, True, True)

        def dx_passes(g, t, h, chunks):
            return [(feat_major[(g, c, t // 2)], P * (t % 2), w_mx[(c, h)]) for c in chunks]

        def dx_mm(g, t):
            for h in range(2):
                bank = take_bank(mm_ring)[0]
                sums[("dx", g, t, h)] = bank
                passes_into(bank, dx_passes(g, t, h, (VV, KK, QA, QB)), E5, E4, True, True)

        def empty(key, engs, dst):
            res = work.tile([P, 1024], F32, name="res", tag="res", bufs=5)
            for a in range(2):
                if key[0] == "dw" and key[1] != VV:
                    copy(engs[a], res[:, 512 * a:512 * (a + 1)].rearrange("p (m u e) -> p m u e", u=2, e=2),
                         sums[key + (a,)][:].rearrange("p (u m e) -> p m u e", u=2, e=2))
                else:
                    copy(engs[a], res[:, 512 * a:512 * (a + 1)], sums[key + (a,)][:])
            nc.sync.dma_start(out=dst, in_=res[:].rearrange("p (a n) -> p a n", a=2))

        def dw_out(c, d2, engs="ss"):
            empty(("dw", c, d2), engs, dw_dst[c][256 * d2:256 * (d2 + 1), :].rearrange("(a p) n -> p a n", p=P))

        def dx_out(g, t, engs="ss"):
            empty(("dx", g, t), engs,
                  out_0[0, 512 * g:512 * (g + 1), :].rearrange("(p t) (a n) -> p t a n", t=4, a=2)[:, t, :, :])

        def dw(c, d2, engs="ss"):
            dw_mm(c, d2)
            dw_out(c, d2, engs)

        def dx(g, t, engs="ss"):
            dx_mm(g, t)
            dx_out(g, t, engs)

        results = {}

        def dw1(c, dt):
            bank = take_bank(mm_ring)[0]
            sums[("dw", c, dt // 2, dt % 2)] = bank
            passes_into(bank, [(x_mx[(g, dt // 4)], P * (dt % 4), tok_major[(g, c)]) for g in range(2)], E4, E5, True, True)

        def cp(kind, c, dt):
            d2, a = dt // 2, dt % 2
            if a == 0:
                results[(c, d2)] = work.tile([P, 1024], F32, name="res", tag="res", bufs=5)
            res = results[(c, d2)]
            copy("s", res[:, 512 * a:512 * (a + 1)], sums[(kind, c, d2, a)][:])
            if a == 1:
                nc.sync.dma_start(out=dw_dst[c][256 * d2:256 * (d2 + 1), :].rearrange("(a p) n -> p a n", p=P),
                                  in_=res[:].rearrange("p (a n) -> p a n", a=2))

        held = {}

        def dx_open(g, t, chunks):
            for h in range(2):
                first = (g, t, h) not in held
                if first:
                    sums[("dx", g, t, h)], held[(g, t, h)] = take_bank(mm_ring, hold=True)
                passes_into(sums[("dx", g, t, h)], dx_passes(g, t, h, chunks), E5, E4, first, False)

        def dx_close(g, t, chunks, engs="ss"):
            for h in range(2):
                passes_into(sums[("dx", g, t, h)], dx_passes(g, t, h, chunks), E5, E4, False, True)
                mm_ring.append(held[(g, t, h)])
            dx_out(g, t, engs)

        load_g(0, KK)
        load_x(0)
        load_vraw(0)
        load_x(1)
        load_vraw(1)
        load_g(1, KK)
        load_wv()
        tables()
        weave_x("s", 0, 0)
        weave_x("s", 0, 1)
        mult(0, KK, 0)
        mult(0, KK, 1)
        mult(0, KK, 2)
        add(0, KK, 0)
        mult(0, KK, 3)
        load_wk()
        load_g(0, QA)
        load_wq(0)
        q_x(0, 0)
        weave_x("s", 1, 0)
        weave_v("v", 0)
        load_g(0, QB)
        load_wq(1)
        load_v(0)
        q_x(0, 1)
        weave_v("s", 1)
        load_g(1, QA)
        q_a(0, VV)
        add(0, KK, 1)
        q_x(1, 0)
        weave_x("s", 1, 1)
        mult(1, KK, 0)
        q_a(1, VV)
        turn_w(VV, 0)
        dw1(VV, 0)
        dw1(VV, 1)
        weave_dz("s", 0, KK)
        mult(1, KK, 1)
        q_x(1, 1)
        add(1, KK, 0)
        turn_w(VV, 1)
        dw1(VV, 2)
        cp("dw", VV, 0)
        cp("dw", VV, 1)
        dw1(VV, 3)
        mult(1, KK, 2)
        q_w(VV, 0)
        mult(1, KK, 3)
        load_g(1, QB)
        load_v(1)
        q_a(0, KK)
        turn_w(KK, 0)
        cp("dw", VV, 2)
        cp("dw", VV, 3)
        dw1(VV, 4)
        dw1(VV, 5)
        add(1, KK, 1)
        q_w(VV, 1)
        weave_dz("v", 1, KK)
        turn_w(KK, 1)
        cp("dw", VV, 4)
        cp("dw", VV, 5)
        dw1(VV, 6)
        dw1(VV, 7)
        q_w(KK, 0)
        q_a(1, KK)
        mult(0, QA, 0)
        turn_w(QA, 0)
        cp("dw", VV, 6)
        cp("dw", VV, 7)
        dw_mm(KK, 0)
        turn_dz(0, KK, 0)
        turn_dz(0, KK, 1)
        mult(0, QA, 1)
        q_w(KK, 1)
        add(0, QA, 0)
        dw_out(KK, 0)
        turn_w(QB, 0)
        dw_mm(KK, 1)
        q_w(QA, 0)
        mult(0, QB, 0)
        q_b(0, KK, 0)
        q_b(0, KK, 1)
        turn_w(QA, 1)
        dw_out(KK, 1)
        dw_mm(KK, 2)
        mult(0, QB, 1)
        q_w(QB, 0)
        turn_dz(0, QA, 0)
        turn_dz(0, VV, 0)
        turn_w(QB, 1)
        dw_out(KK, 2)
        add(0, QB, 0)
        turn_dz(0, QB, 0)
        dw_mm(KK, 3)
        turn_dz(0, VV, 1)
        q_w(QA, 1)
        mult(0, QA, 2)
        q_b(0, QA, 0)
        q_b(0, VV, 0)
        mult(0, QA, 3)
        q_w(QB, 1)
        q_b(0, QB, 0)
        add(0, QA, 1)
        dw_out(KK, 3)
        dx_mm(0, 0)
        turn_dz(0, QA, 1)
        dx_out(0, 0)
        dx(0, 1)
        mult(0, QB, 2)
        q_b(0, VV, 1)
        mult(0, QB, 3)
        q_b(0, QA, 1)
        add(0, QB, 1)
        turn_dz(0, QB, 1)
        turn_dz(1, KK, 0)
        turn_dz(1, VV, 0)
        weave_dz("s", 0, QA)
        mult(1, QA, 0)
        q_b(0, QB, 1)
        dx(0, 2)
        dx(0, 3)
        mult(1, QA, 1)
        q_b(1, KK, 0)
        q_b(1, VV, 0)
        add(1, QA, 0)
        turn_dz(1, QA, 0)
        turn_dz(1, KK, 1)
        turn_dz(1, VV, 1)
        weave_dz("s", 0, QB)
        dx_open(1, 0, [VV, KK])
        dx_open(1, 1, [VV, KK])
        mult(1, QA, 2)
        q_a(0, QA)
        mult(1, QA, 3)
        q_b(1, QA, 0)
        dx_open(1, 0, [QA])
        dx_open(1, 1, [QA])
        add(1, QA, 1)
        turn_dz(1, QA, 1)
        q_b(1, KK, 1)
        weave_dz("v", 1, QA)
        q_b(1, VV, 1)
        q_a(1, QA)
        dw(QA, 0)
        dw(QA, 1)
        dw(QA, 2)
        mult(1, QB, 0)
        mult(1, QB, 1)
        q_b(1, QA, 1)
        add(1, QB, 0)
        turn_dz(1, QB, 0)
        dw(QA, 3)
        mult(1, QB, 2)
        q_b(1, QB, 0)
        dx_close(1, 0, [QB])
        dx_close(1, 1, [QB])
        dx_open(1, 2, [VV, KK, QA])
        mult(1, QB, 3)
        q_a(0, QB)
        add(1, QB, 1)
        turn_dz(1, QB, 1)
        dx_open(1, 3, [VV, KK, QA])
        weave_dz("v", 1, QB)
        q_b(1, QB, 1)
        q_a(1, QB)
        dx_close(1, 2, [QB], "vs")
        dx_close(1, 3, [QB], "vs")
        for d2 in range(4):
            dw(QB, d2, "vs")
